import numpy as np
import ml_dtypes


def mxq(x, axis, fmt="e4m3"):
    dtype, down = {"e4m3": (ml_dtypes.float8_e4m3fn, 7), "e5m2": (ml_dtypes.float8_e5m2, 14)}[fmt]
    v = np.moveaxis(np.asarray(x, np.float32).astype(ml_dtypes.bfloat16).astype(np.float64), axis, -1)
    blocks = v.reshape(v.shape[:-1] + (-1, 32))
    amax = np.abs(blocks).max(-1, keepdims=True)
    byte = np.maximum(np.where(amax > 0, np.frexp(amax)[1] - 1 + 127, 0) - down, 1)
    scale = np.exp2(byte - 127.0)
    codes = (blocks / scale).astype(np.float32).astype(dtype).astype(np.float64)
    return np.moveaxis((codes * scale).reshape(v.shape), -1, axis)


WIDE = False


def mx_kscale(k):
    if not WIDE:
        return np.ones(k)
    levels = np.array([10, -10, 5, -5, 0])
    if k % 512:
        return np.exp2(np.random.permutation(np.resize(levels, k // 32))).repeat(32)
    a = np.empty((k // 512, 16))
    for p in range(k // 512):
        a[p, :8] = np.random.permutation(np.resize(levels, 8))
        for g in range(8):
            far = levels[np.abs(levels - a[p, g]) >= 10]
            a[p, g + 8] = far[np.random.randint(len(far))]
    return np.exp2(a.ravel()).repeat(32)


BF16 = ml_dtypes.bfloat16


def bf(x):
    return np.asarray(x, np.float32).astype(BF16)


def f64(x):
    return np.asarray(x).astype(np.float64)


N, I0, O0, I1, O1, I2, O2, D0, D1, D2 = 1024, 512, 512, 256, 256, 128, 128, 1, 3, 5


def irrep_linear(x, w):
    return (x.transpose(2, 0, 1) @ w.transpose(2, 1, 0)).transpose(1, 2, 0)


def setup_inputs():
    s = mx_kscale(I0)
    return {"x0e": bf(np.random.standard_normal((N, I0, D0)) * s[None, :, None]),
            "x1o": bf(np.random.standard_normal((N, I1, D1))),
            "x2e": bf(np.random.standard_normal((N, I2, D2))),
            "w0e": bf(np.random.standard_normal((O0, I0, D0)) / np.sqrt(I0) / s[None, :, None]),
            "w1o": bf(np.random.standard_normal((O1, I1, D1)) / np.sqrt(I1)),
            "w2e": bf(np.random.standard_normal((O2, I2, D2)) / np.sqrt(I2)),
            "bias": bf(np.random.standard_normal(O0) * 0.5)}


def core(x0e, x1o, x2e, w0e, w1o, w2e, bias):
    y0e = irrep_linear(mxq(f64(x0e), 1, "e4m3"), mxq(f64(w0e), 1, "e4m3")) + f64(bias)[None, :, None]
    y1o = irrep_linear(f64(x1o), f64(w1o))
    y2e = irrep_linear(f64(x2e), f64(w2e))
    n = x0e.shape[0]
    return np.concatenate([y0e.reshape(n, -1), y1o.reshape(n, -1), y2e.reshape(n, -1)], axis=-1)


def e4m3fn_bytes(y):
    return np.clip(np.asarray(y, np.float64), -448.0, 448.0).astype(np.float32).astype(ml_dtypes.float8_e4m3fn).view(np.uint8)


def reference(x0e, x1o, x2e, w0e, w1o, w2e, bias):
    out = core(x0e, x1o, x2e, w0e, w1o, w2e, bias)
    s = np.max(np.abs(out), axis=-1, keepdims=True) / 448.0
    return out, e4m3fn_bytes(out / s)

@@ -1,0 +1,394 @@
+from contextlib import ExitStack
+
+import concourse.mybir as mybir
+from concourse.masks import make_identity
+
+F32 = mybir.dt.float32
+BF16 = mybir.dt.bfloat16
+U32 = mybir.dt.uint32
+U8 = mybir.dt.uint8
+FP8X4 = mybir.dt.float8_e4m3fn_x4
+FP8 = mybir.dt.float8_e4m3fn
+ALU = mybir.AluOpType
+ACT = mybir.ActivationFunctionType
+AX = mybir.AxisListType
+
+P = 128
+NT = 8
+FLOPS = 2 * 1024 * (512 * 512 + 3 * 256 * 256 + 5 * 128 * 128)
+CVS = (1536, 1088, 896, 896, 896, 416, 0, 1280)
+PIECES = (2, 1, 1, 1, 1, 1, 1, 2)
+CHUNKS = ((0, 1), (1, 2), (2, 4), (4, 6), (6, 8))
+CHUNKS0 = ((0, 2), (2, 4), (4, 6), (6, 8))
+
+
+def tile_linearlayer_kernel(tc, x0e, x1o, x2e, w0e, w1o, w2e, bias, out_0, out_1):
+    nc = tc.nc
+    with ExitStack() as ctx:
+        const = ctx.enter_context(tc.tile_pool(name="const", bufs=1))
+        xin = ctx.enter_context(tc.tile_pool(name="xin", bufs=1))
+        xt = ctx.enter_context(tc.tile_pool(name="xt", bufs=4))
+        res = ctx.enter_context(tc.tile_pool(name="res", bufs=6))
+        psum = ctx.enter_context(tc.psum_pool(name="psum", bufs=1))
+        ctx.enter_context(tc.manual_schedule())
+
+        x0v = x0e.rearrange("(p t) i o -> p t (i o)", t=NT)
+        x1v = x1o.rearrange("(p t) i m -> p t (i m)", t=NT)
+        x2v = x2e.rearrange("(p t) i m -> p t (i m)", t=NT)
+        o0v = out_0.rearrange("(p t) c -> p t c", t=NT)
+        o1v = out_1.rearrange("(p t) c -> p t c", t=NT)
+
+        def copy(eng, out, in_):
+            if eng == "V":
+                nc.vector.tensor_copy(out=out, in_=in_)
+            else:
+                nc.scalar.copy(out=out, in_=in_)
+
+        def words(ap3):
+            return ap3.rearrange("p a n -> p (a n)").bitcast(F32)
+
+        zero = const.tile([P, 1], F32, name="zero")
+        nc.vector.memset(zero[:], 0.0)
+        junk = const.tile([P, 1], F32, name="junk")
+        nc.scalar.activation(out=junk[:], in_=zero[:], func=ACT.Identity, bias=zero[:, 0:1], scale=zero[:, 0:1])
+        ones = const.tile([P, P], BF16, name="ones")
+        nc.vector.memset(ones[:], 1.0)
+        brow = const.tile([P, 512], BF16, name="brow")
+        nc.vector.memset(brow[:], 0.0)
+        identf = const.tile([P, P], F32, name="identf")
+        make_identity(nc, identf[:])
+        identb = const.tile([P, P], BF16, name="identb")
+        make_identity(nc, identb[:])
+
+        pwm = psum.tile([P, 512], F32, name="pwm", tag="b7")
+        nc.tensor.matmul(pwm[:], lhsT=ones[:], rhs=brow[:], start=True, stop=True)
+        nc.tensor.matmul(pwm[:], lhsT=ones[:], rhs=brow[:], start=True, stop=True)
+        nc.tensor.matmul(pwm[:, 0:256], lhsT=ones[:], rhs=brow[:, 0:256], start=True, stop=True)
+
+        x0s, x1s, x2s = {}, {}, {}
+
+        def load_x(c, which):
+            a, b = CHUNKS0[c] if which == 0 else CHUNKS[c]
+            view, width, dst = ((x0v, 512, x0s), (x1v, 768, x1s), (x2v, 640, x2s))[which]
+            tl = xin.tile([P, b - a, width], BF16, name="x%dc%d" % (which, c))
+            nc.sync.dma_start(out=tl[:], in_=view[:, a:b, :])
+            for t in range(a, b):
+                dst[t] = tl[:, t - a, :]
+
+        w0v = w0e.rearrange("(j p) i o -> p j (i o)", p=P)
+        w0a = const.tile([P, 2, 512], BF16, name="w0a")
+        nc.sync.dma_start(out=w0a[:], in_=w0v[:, 0:2, :])
+        w0b = const.tile([P, 2, 512], BF16, name="w0b")
+        nc.sync.dma_start(out=w0b[:], in_=w0v[:, 2:4, :])
+        load_x(0, 0)
+        nc.sync.dma_start(out=brow[0:1, :], in_=bias.rearrange("(a n) -> a n", a=1))
+        w1 = const.tile([P, 2, 768], BF16, name="w1")
+        nc.sync.dma_start(out=w1[:], in_=w1o.rearrange("(j p) i m -> p j (i m)", p=P))
+        load_x(0, 1)
+        w2 = const.tile([P, 640], BF16, name="w2")
+        nc.sync.dma_start(out=w2[:], in_=w2e.rearrange("p i m -> p (i m)"))
+        load_x(0, 2)
+        load_x(1, 1)
+        load_x(1, 2)
+        for c in range(2, len(CHUNKS)):
+            load_x(c - 1, 0)
+            load_x(c, 1)
+            load_x(c, 2)
+
+        bias32 = const.tile([P, 512], F32, name="bias32")
+
+        def bias_stage():
+            pb = psum.tile([P, 512], F32, name="pb", tag="b0")
+            nc.tensor.matmul(pb[:], lhsT=ones[:], rhs=brow[:], start=True, stop=True)
+            nc.scalar.copy(out=bias32[:], in_=pb[:])
+
+        wg = const.tile([P, 512, 4], BF16, name="wg", align_bytes=64)
+        wcodes = const.tile([P, 512], U32, name="wcodes", align_bytes=64)
+        wscales = const.tile([P, 512], U8, name="wscales", align_bytes=64)
+
+        def w0_stage(b, w0h, eng, bank):
+            pw = psum.tile([P, 2, 2, P], F32, name="pw%d" % b, tag=bank)
+            for j in range(2):
+                wd = w0h[:, j, :].bitcast(F32)
+                for u in range(2):
+                    nc.tensor.transpose(pw[:, j, u, :], wd[:, u:256:2], identf[:])
+            dst = wg[:, 256 * b : 256 * (b + 1), :].bitcast(F32).rearrange("p (j o) u -> p j o u", j=2)
+            copy(eng, dst, pw[:].rearrange("p j u o -> p j o u"))
+            nc.vector.quantize_mx(
+                out=wcodes[:, 256 * b : 256 * (b + 1)].bitcast(FP8X4),
+                scales=wscales[:, 256 * b : 256 * (b + 1)],
+                in_=wg[:, 256 * b : 256 * (b + 1), :].rearrange("p n j -> p (n j)"),
+            )
+
+        wT1 = const.tile([P, 6, 256], BF16, name="wT1")
+
+        def w1_stage(j, eng, bank):
+            pw1 = psum.tile([P, 6, P], BF16, name="pw1_%d" % j, tag=bank)
+            for m in range(3):
+                for kk in range(2):
+                    nc.tensor.transpose(pw1[:, 2 * m + kk, :], w1[:, j, 384 * kk + m : 384 * (kk + 1) : 3], identb[:])
+            copy(eng, wT1[:, :, 128 * j : 128 * (j + 1)].bitcast(F32), pw1[:].bitcast(F32))
+
+        wT2 = const.tile([P, 5, P], BF16, name="wT2")
+
+        def w2_stage(eng, bank):
+            pw2 = psum.tile([P, 5, P], BF16, name="pw2", tag=bank)
+            for m in range(5):
+                nc.tensor.transpose(pw2[:, m, :], w2[:, m:640:5], identb[:])
+            copy(eng, words(wT2[:]), words(pw2[:]))
+
+        p0s, p1s, p2s, g0s, xcs, xss, xT1s, xT2s = {}, {}, {}, {}, {}, {}, {}, {}
+        ps0s, ps1s, ps2s, o32s, ams, rs, o8s = {}, {}, {}, {}, {}, {}, {}
+
+        def x0_pe(t):
+            if t % 2:
+                return
+            p0 = psum.tile([P, 2, 2, P], F32, name="p0", tag="b5")
+            for j in range(2):
+                wd = x0s[t + j].bitcast(F32)
+                for u in range(2):
+                    nc.tensor.transpose(p0[:, j, u, :], wd[:, u:256:2], identf[:])
+            p0s[t] = p0
+
+        def x0_cp(t, eng):
+            if t % 2:
+                return
+            g0 = xt.tile([P, 2 * P, 4], BF16, name="g0", align_bytes=64)
+            copy(
+                eng,
+                g0[:].bitcast(F32).rearrange("p (j n) u -> p j n u", j=2),
+                p0s.pop(t)[:].rearrange("p j u n -> p j n u"),
+            )
+            g0s[t] = g0
+
+        def quant(t):
+            if t % 2:
+                return
+            xc = xt.tile([P, 2 * P], U32, name="xc", align_bytes=64)
+            xs = xt.tile([P, 2 * P], U8, name="xs", align_bytes=64)
+            nc.vector.quantize_mx(
+                out=xc[:].bitcast(FP8X4), scales=xs[:], in_=g0s.pop(t)[:].rearrange("p n j -> p (n j)")
+            )
+            for j in range(2):
+                xcs[t + j] = xc[:, P * j : P * (j + 1)]
+                xss[t + j] = xs[:, P * j : P * (j + 1)]
+
+        def x1_pe(t):
+            p1 = psum.tile([P, 6, P], BF16, name="p1", tag="b6")
+            for m in range(3):
+                for kk in range(2):
+                    nc.tensor.transpose(p1[:, 2 * m + kk, :], x1s[t][:, 384 * kk + m : 384 * (kk + 1) : 3], identb[:])
+            p1s[t] = p1
+
+        def x1_cp(t, eng):
+            xT1 = xt.tile([P, 6, P], BF16, name="xT1")
+            copy(eng, words(xT1[:]), words(p1s.pop(t)[:]))
+            xT1s[t] = xT1
+
+        def x2_pe(t):
+            p2 = psum.tile([P, 5, P], BF16, name="p2", tag="b7")
+            for m in range(5):
+                nc.tensor.transpose(p2[:, m, :], x2s[t][:, m:640:5], identb[:])
+            p2s[t] = p2
+
+        def x2_cp(t, eng):
+            xT2 = xt.tile([P, 5, P], BF16, name="xT2")
+            copy(eng, words(xT2[:]), words(p2s.pop(t)[:]))
+            xT2s[t] = xT2
+
+        def m0(t):
+            ps0 = psum.tile([P, 512], F32, name="ps0", tag="b0")
+            nc.tensor.matmul_mx(
+                out=ps0[:],
+                lhsT=xcs.pop(t).bitcast(FP8X4),
+                lhsT_scale=xss.pop(t),
+                rhs=wcodes[:].bitcast(FP8X4),
+                rhs_scale=wscales[:],
+                start=True,
+                stop=True,
+            )
+            ps0s[t] = ps0
+
+        def m1(t):
+            xT1 = xT1s.pop(t)
+            pa = psum.tile([P, 3, P], F32, name="ps1a", tag="b1")
+            pbk = psum.tile([P, 3, P], F32, name="ps1b", tag="b2")
+            ps1 = (pa, pbk)
+            for m in range(3):
+                for kk in range(2):
+                    for h in range(2):
+                        nc.tensor.matmul(
+                            ps1[h][:, m, :],
+                            lhsT=xT1[:, 2 * m + kk, :],
+                            rhs=wT1[:, 2 * m + kk, 128 * h : 128 * (h + 1)],
+                            start=(kk == 0),
+                            stop=(kk == 1),
+                        )
+            ps1s[t] = ps1
+
+        def m2(t):
+            xT2 = xT2s.pop(t)
+            pa = psum.tile([P, 5, 64], F32, name="ps2a", tag="b3")
+            pbk = psum.tile([P, 5, 64], F32, name="ps2b", tag="b4")
+            ps2 = (pa, pbk)
+            for m in range(5):
+                for h in range(2):
+                    nc.tensor.matmul(
+                        ps2[h][:, m, :],
+                        lhsT=xT2[:, m, :],
+                        rhs=wT2[:, m, 64 * h : 64 * (h + 1)],
+                        start=True,
+                        stop=True,
+                    )
+            ps2s[t] = ps2
+
+        def new_out(t):
+            o32 = res.tile([P, 1920], F32, name="o32")
+            o32s[t] = o32
+            am = res.tile([P, 2], F32, name="am")
+            ams[t] = am
+
+        def a0(t):
+            nc.vector.tensor_tensor(out=o32s[t][:, 0:512], in0=ps0s.pop(t)[:], in1=bias32[:], op=ALU.add)
+
+        def a1(t, h, eng):
+            copy(
+                eng,
+                o32s[t][:, 512 + 384 * h : 512 + 384 * (h + 1)].rearrange("p (o m) -> p o m", m=3),
+                ps1s[t][h][:].rearrange("p m o -> p o m"),
+            )
+
+        def a2(t, h, eng):
+            copy(
+                eng,
+                o32s[t][:, 1280 + 320 * h : 1280 + 320 * (h + 1)].rearrange("p (o m) -> p o m", m=5),
+                ps2s[t][h][:].rearrange("p m o -> p o m"),
+            )
+
+        def st0(t):
+            nc.sync.dma_start(out=o0v[:, t, :], in_=o32s[t][:])
+
+        def red(t, piece):
+            lo, hi = ((0, 1280), (1280, 1920))[piece] if PIECES[t] == 2 else (0, 1920)
+            nc.vector.tensor_reduce(
+                out=ams[t][:, piece : piece + 1],
+                in_=o32s[t][:, lo:hi],
+                axis=AX.X,
+                op=ALU.max,
+                apply_absolute_value=True,
+            )
+
+        def factor(t):
+            n = PIECES[t]
+            rc = res.tile([P, 2], F32, name="rc")
+            nc.vector.reciprocal(out=rc[:, 0:n], in_=ams.pop(t)[:, 0:n])
+            r = res.tile([P, 1], F32, name="r")
+            if n == 2:
+                nc.gpsimd.tensor_scalar(
+                    out=r[:], in0=rc[:, 0:1], scalar1=rc[:, 1:2], scalar2=448.0, op0=ALU.min, op1=ALU.mult
+                )
+            else:
+                nc.gpsimd.tensor_scalar(
+                    out=r[:], in0=rc[:, 0:1], scalar1=448.0, scalar2=0.0, op0=ALU.mult, op1=ALU.add
+                )
+            rs[t] = r
+            o8 = res.tile([P, 1920], FP8, name="o8")
+            o8s[t] = o8
+
+        def cast_v(t):
+            cv = CVS[t]
+            if cv == 0:
+                return
+            nc.vector.tensor_scalar(
+                out=o8s[t][:, 0:cv],
+                in0=o32s[t][:, 0:cv],
+                scalar1=rs[t][:, 0:1],
+                scalar2=None,
+                op0=ALU.mult,
+                saturate=False,
+            )
+
+        def cast_s(t):
+            cv = CVS[t]
+            nc.scalar.activation(
+                out=o8s[t][:, cv:1920],
+                in_=o32s[t][:, cv:1920],
+                func=ACT.Identity,
+                bias=zero[:, 0:1],
+                scale=rs[t][:, 0:1],
+                saturate=False,
+            )
+
+        def st1(t):
+            nc.sync.dma_start(out=o1v[:, t, :], in_=o8s.pop(t)[:].bitcast(U8))
+
+        w0_stage(0, w0a, "V", "b1")
+        w0_stage(1, w0b, "S", "b2")
+        x0_pe(0)
+        x0_cp(0, "S")
+        quant(0)
+        bias_stage()
+        w1_stage(0, "V", "b3")
+        w1_stage(1, "S", "b4")
+        x1_pe(0)
+        x1_cp(0, "S")
+        w2_stage("S", "b5")
+        x2_pe(0)
+        x2_cp(0, "V")
+        new_out(0)
+        m0(0)
+        a0(0)
+        m1(0)
+        a1(0, 0, "S")
+        a1(0, 1, "V")
+        x0_pe(1)
+        x0_cp(1, "S")
+        quant(1)
+        m2(0)
+        a2(0, 0, "S")
+        a2(0, 1, "V")
+        st0(0)
+        x1_pe(1)
+        x1_cp(1, "S")
+        x2_pe(1)
+        x2_cp(1, "S")
+        red(0, 0)
+        for t in range(1, NT):
+            if t + 1 < NT:
+                x0_pe(t + 1)
+                x1_pe(t + 1)
+                x2_pe(t + 1)
+            new_out(t)
+            m1(t)
+            m0(t)
+            m2(t)
+            if t >= 2:
+                cast_s(t - 2)
+                st1(t - 2)
+            if t + 1 < NT:
+                x0_cp(t + 1, "S")
+                x1_cp(t + 1, "S")
+                x2_cp(t + 1, "S")
+            if t >= 2:
+                red(t - 1, 0)
+            if PIECES[t - 1] == 2:
+                red(t - 1, 1)
+            factor(t - 1)
+            if t + 1 < NT:
+                quant(t + 1)
+            helper = "S"
+            a1(t, 0, "S")
+            a1(t, 1, "S")
+            a0(t)
+            a2(t, 0, "S")
+            a2(t, 1, helper)
+            st0(t)
+            cast_v(t - 1)
+        cast_s(NT - 2)
+        st1(NT - 2)
+        red(NT - 1, 0)
+        red(NT - 1, 1)
+        factor(NT - 1)
+        cast_v(NT - 1)
+        cast_s(NT - 1)
+        st1(NT - 1)

@@ -55,15 +55,17 @@ def tile_linearlayer_kernel(tc, x0e, x1o, x2e, w0e, w1o, w2e, bias, out_0, out_1
         nc.vector.memset(ones[:], 1.0)
         brow = const.tile([P, 512], BF16, name="brow")
         nc.vector.memset(brow[:], 0.0)
+        wz = const.tile([P, 512], BF16, name="wz")
+        nc.vector.memset(wz[:], 0.0)
         identf = const.tile([P, P], F32, name="identf")
         make_identity(nc, identf[:])
         identb = const.tile([P, P], BF16, name="identb")
         make_identity(nc, identb[:])
 
         pwm = psum.tile([P, 512], F32, name="pwm", tag="b7")
-        nc.tensor.matmul(pwm[:], lhsT=ones[:], rhs=brow[:], start=True, stop=True)
-        nc.tensor.matmul(pwm[:], lhsT=ones[:], rhs=brow[:], start=True, stop=True)
-        nc.tensor.matmul(pwm[:, 0:256], lhsT=ones[:], rhs=brow[:, 0:256], start=True, stop=True)
+        nc.tensor.matmul(pwm[:], lhsT=ones[:], rhs=wz[:], start=True, stop=True)
+        nc.tensor.matmul(pwm[:], lhsT=ones[:], rhs=wz[:], start=True, stop=True)
+        nc.tensor.matmul(pwm[:, 0:256], lhsT=ones[:], rhs=wz[:, 0:256], start=True, stop=True)
 
         x0s, x1s, x2s = {}, {}, {}
 

@@ -53,10 +53,15 @@ def tile_linearlayer_kernel(tc, x0e, x1o, x2e, w0e, w1o, w2e, bias, out_0, out_1
         nc.scalar.activation(out=junk[:], in_=zero[:], func=ACT.Identity, bias=zero[:, 0:1], scale=zero[:, 0:1])
         ones = const.tile([P, P], BF16, name="ones")
         nc.vector.memset(ones[:], 1.0)
-        brow = const.tile([P, 512], BF16, name="brow")
-        nc.vector.memset(brow[:], 0.0)
         wz = const.tile([P, 512], BF16, name="wz")
         nc.vector.memset(wz[:], 0.0)
+        cst = const.tile([P, 512], BF16, name="cst", align_bytes=64)
+        nc.vector.memset(cst[:], 1.0)
+        ccodes = const.tile([P, P], U32, name="ccodes", align_bytes=64)
+        cscales = const.tile([P, P], U8, name="cscales", align_bytes=64)
+        nc.vector.quantize_mx(out=ccodes[:].bitcast(FP8X4), scales=cscales[:], in_=cst[:])
+        brow = const.tile([P, 512], BF16, name="brow")
+        nc.vector.memset(brow[:], 0.0)
         identf = const.tile([P, P], F32, name="identf")
         make_identity(nc, identf[:])
         identb = const.tile([P, P], BF16, name="identb")
@@ -66,6 +71,16 @@ def tile_linearlayer_kernel(tc, x0e, x1o, x2e, w0e, w1o, w2e, bias, out_0, out_1
         nc.tensor.matmul(pwm[:], lhsT=ones[:], rhs=wz[:], start=True, stop=True)
         nc.tensor.matmul(pwm[:], lhsT=ones[:], rhs=wz[:], start=True, stop=True)
         nc.tensor.matmul(pwm[:, 0:256], lhsT=ones[:], rhs=wz[:, 0:256], start=True, stop=True)
+        for k in range(8):
+            nc.tensor.matmul_mx(
+                out=pwm[:, 0:P],
+                lhsT=ccodes[:].bitcast(FP8X4),
+                lhsT_scale=cscales[:],
+                rhs=ccodes[:].bitcast(FP8X4),
+                rhs_scale=cscales[:],
+                start=True,
+                stop=True,
+            )
 
         x0s, x1s, x2s = {}, {}, {}
 

@@ -94,7 +94,8 @@ def tile_linearlayer_kernel(tc, x0e, x1o, x2e, w0e, w1o, w2e, bias, out_0, out_1
 
         w0v = w0e.rearrange("(j p) i o -> p j (i o)", p=P)
         w0a = const.tile([P, 2, 512], BF16, name="w0a")
-        nc.sync.dma_start(out=w0a[:], in_=w0v[:, 0:2, :])
+        nc.sync.dma_start(out=w0a[:, 0:1, :], in_=w0v[:, 0:1, :])
+        nc.sync.dma_start(out=w0a[:, 1:2, :], in_=w0v[:, 1:2, :])
         w0b = const.tile([P, 2, 512], BF16, name="w0b")
         nc.sync.dma_start(out=w0b[:], in_=w0v[:, 2:4, :])
         load_x(0, 0)
@@ -300,7 +301,11 @@ def tile_linearlayer_kernel(tc, x0e, x1o, x2e, w0e, w1o, w2e, bias, out_0, out_1
             rc = res.tile([P, 2], F32, name="rc")
             nc.vector.reciprocal(out=rc[:, 0:n], in_=ams.pop(t)[:, 0:n])
             r = res.tile([P, 1], F32, name="r")
-            if n == 2:
+            if t == NT - 1:
+                nc.vector.tensor_scalar(
+                    out=r[:], in0=rc[:, 0:1], scalar1=rc[:, 1:2], scalar2=448.0, op0=ALU.min, op1=ALU.mult
+                )
+            elif n == 2:
                 nc.gpsimd.tensor_scalar(
                     out=r[:], in0=rc[:, 0:1], scalar1=rc[:, 1:2], scalar2=448.0, op0=ALU.min, op1=ALU.mult
                 )

@@ -180,16 +180,16 @@ def tile_linearlayer_kernel(tc, x0e, x1o, x2e, w0e, w1o, w2e, bias, out_0, out_1
             g0s[t] = g0
 
         def quant(t):
-            if t % 2:
-                return
-            xc = xt.tile([P, 2 * P], U32, name="xc", align_bytes=64)
-            xs = xt.tile([P, 2 * P], U8, name="xs", align_bytes=64)
+            xc = xt.tile([P, P], U32, name="xc", align_bytes=64)
+            xs = xt.tile([P, P], U8, name="xs", align_bytes=64)
+            g0 = g0s[t - t % 2]
             nc.vector.quantize_mx(
-                out=xc[:].bitcast(FP8X4), scales=xs[:], in_=g0s.pop(t)[:].rearrange("p n j -> p (n j)")
+                out=xc[:].bitcast(FP8X4),
+                scales=xs[:],
+                in_=g0[:, P * (t % 2) : P * (t % 2 + 1), :].rearrange("p n j -> p (n j)"),
             )
-            for j in range(2):
-                xcs[t + j] = xc[:, P * j : P * (j + 1)]
-                xss[t + j] = xs[:, P * j : P * (j + 1)]
+            xcs[t] = xc[:]
+            xss[t] = xs[:]
 
         def x1_pe(t):
             p1 = psum.tile([P, 6, P], BF16, name="p1", tag="b6")
@@ -395,9 +395,9 @@ def tile_linearlayer_kernel(tc, x0e, x1o, x2e, w0e, w1o, w2e, bias, out_0, out_1
                 red(t - 1, 0)
             if PIECES[t - 1] == 2:
                 red(t - 1, 1)
-            factor(t - 1)
             if t + 1 < NT:
                 quant(t + 1)
+            factor(t - 1)
             helper = "S"
             a1(t, 0, "S")
             a1(t, 1, "S")

@@ -397,11 +397,14 @@ def tile_linearlayer_kernel(tc, x0e, x1o, x2e, w0e, w1o, w2e, bias, out_0, out_1
                 red(t - 1, 1)
             if t + 1 < NT:
                 quant(t + 1)
+            else:
+                a0(t)
             factor(t - 1)
             helper = "S"
             a1(t, 0, "S")
             a1(t, 1, "S")
-            a0(t)
+            if t + 1 < NT:
+                a0(t)
             a2(t, 0, "S")
             a2(t, 1, helper)
             st0(t)

@@ -384,13 +384,13 @@ def tile_linearlayer_kernel(tc, x0e, x1o, x2e, w0e, w1o, w2e, bias, out_0, out_1
             m1(t)
             m0(t)
             m2(t)
-            if t >= 2:
-                cast_s(t - 2)
-                st1(t - 2)
             if t + 1 < NT:
                 x0_cp(t + 1, "S")
                 x1_cp(t + 1, "S")
                 x2_cp(t + 1, "S")
+            if t >= 2:
+                cast_s(t - 2)
+                st1(t - 2)
             if t >= 2:
                 red(t - 1, 0)
             if PIECES[t - 1] == 2:

@@ -287,7 +287,7 @@ def tile_linearlayer_kernel(tc, x0e, x1o, x2e, w0e, w1o, w2e, bias, out_0, out_1
             nc.sync.dma_start(out=o0v[:, t, :], in_=o32s[t][:])
 
         def red(t, piece):
-            lo, hi = ((0, 1280), (1280, 1920))[piece] if PIECES[t] == 2 else (0, 1920)
+            lo, hi = (((0, 1280), (1280, 1920)) if t == 0 else ((512, 1920), (0, 512)))[piece] if PIECES[t] == 2 else (0, 1920)
             nc.vector.tensor_reduce(
                 out=ams[t][:, piece : piece + 1],
                 in_=o32s[t][:, lo:hi],

from contextlib import ExitStack

import concourse.mybir as mybir
from concourse.masks import make_identity

F32 = mybir.dt.float32
BF16 = mybir.dt.bfloat16
U32 = mybir.dt.uint32
U8 = mybir.dt.uint8
FP8X4 = mybir.dt.float8_e4m3fn_x4
FP8 = mybir.dt.float8_e4m3fn
ALU = mybir.AluOpType
ACT = mybir.ActivationFunctionType
AX = mybir.AxisListType

P = 128
NT = 8
FLOPS = 2 * 1024 * (512 * 512 + 3 * 256 * 256 + 5 * 128 * 128)
CVS = (1536, 1088, 896, 896, 896, 416, 0, 1280)
PIECES = (2, 1, 1, 1, 1, 1, 1, 2)
CHUNKS = ((0, 1), (1, 2), (2, 4), (4, 6), (6, 8))
CHUNKS0 = ((0, 2), (2, 4), (4, 6), (6, 8))


def tile_linearlayer_kernel(tc, x0e, x1o, x2e, w0e, w1o, w2e, bias, out_0, out_1):
    nc = tc.nc
    with ExitStack() as ctx:
        const = ctx.enter_context(tc.tile_pool(name="const", bufs=1))
        xin = ctx.enter_context(tc.tile_pool(name="xin", bufs=1))
        xt = ctx.enter_context(tc.tile_pool(name="xt", bufs=4))
        res = ctx.enter_context(tc.tile_pool(name="res", bufs=6))
        psum = ctx.enter_context(tc.psum_pool(name="psum", bufs=1))
        ctx.enter_context(tc.manual_schedule())

        x0v = x0e.rearrange("(p t) i o -> p t (i o)", t=NT)
        x1v = x1o.rearrange("(p t) i m -> p t (i m)", t=NT)
        x2v = x2e.rearrange("(p t) i m -> p t (i m)", t=NT)
        o0v = out_0.rearrange("(p t) c -> p t c", t=NT)
        o1v = out_1.rearrange("(p t) c -> p t c", t=NT)

        def copy(eng, out, in_):
            if eng == "V":
                nc.vector.tensor_copy(out=out, in_=in_)
            else:
                nc.scalar.copy(out=out, in_=in_)

        def words(ap3):
            return ap3.rearrange("p a n -> p (a n)").bitcast(F32)

        zero = const.tile([P, 1], F32, name="zero")
        nc.vector.memset(zero[:], 0.0)
        junk = const.tile([P, 1], F32, name="junk")
        nc.scalar.activation(out=junk[:], in_=zero[:], func=ACT.Identity, bias=zero[:, 0:1], scale=zero[:, 0:1])
        ones = const.tile([P, P], BF16, name="ones")
        nc.vector.memset(ones[:], 1.0)
        wz = const.tile([P, 512], BF16, name="wz")
        nc.vector.memset(wz[:], 0.0)
        cst = const.tile([P, 512], BF16, name="cst", align_bytes=64)
        nc.vector.memset(cst[:], 1.0)
        ccodes = const.tile([P, P], U32, name="ccodes", align_bytes=64)
        cscales = const.tile([P, P], U8, name="cscales", align_bytes=64)
        nc.vector.quantize_mx(out=ccodes[:].bitcast(FP8X4), scales=cscales[:], in_=cst[:])
        brow = const.tile([P, 512], BF16, name="brow")
        nc.vector.memset(brow[:], 0.0)
        identf = const.tile([P, P], F32, name="identf")
        make_identity(nc, identf[:])
        identb = const.tile([P, P], BF16, name="identb")
        make_identity(nc, identb[:])

        pwm = psum.tile([P, 512], F32, name="pwm", tag="b7")
        nc.tensor.matmul(pwm[:], lhsT=ones[:], rhs=wz[:], start=True, stop=True)
        nc.tensor.matmul(pwm[:], lhsT=ones[:], rhs=wz[:], start=True, stop=True)
        nc.tensor.matmul(pwm[:, 0:256], lhsT=ones[:], rhs=wz[:, 0:256], start=True, stop=True)
        for k in range(8):
            nc.tensor.matmul_mx(
                out=pwm[:, 0:P],
                lhsT=ccodes[:].bitcast(FP8X4),
                lhsT_scale=cscales[:],
                rhs=ccodes[:].bitcast(FP8X4),
                rhs_scale=cscales[:],
                start=True,
                stop=True,
            )

        x0s, x1s, x2s = {}, {}, {}

        def load_x(c, which):
            a, b = CHUNKS0[c] if which == 0 else CHUNKS[c]
            view, width, dst = ((x0v, 512, x0s), (x1v, 768, x1s), (x2v, 640, x2s))[which]
            tl = xin.tile([P, b - a, width], BF16, name="x%dc%d" % (which, c))
            nc.sync.dma_start(out=tl[:], in_=view[:, a:b, :])
            for t in range(a, b):
                dst[t] = tl[:, t - a, :]

        w0v = w0e.rearrange("(j p) i o -> p j (i o)", p=P)
        w0a = const.tile([P, 2, 512], BF16, name="w0a")
        nc.sync.dma_start(out=w0a[:, 0:1, :], in_=w0v[:, 0:1, :])
        nc.sync.dma_start(out=w0a[:, 1:2, :], in_=w0v[:, 1:2, :])
        w0b = const.tile([P, 2, 512], BF16, name="w0b")
        nc.sync.dma_start(out=w0b[:], in_=w0v[:, 2:4, :])
        load_x(0, 0)
        nc.sync.dma_start(out=brow[0:1, :], in_=bias.rearrange("(a n) -> a n", a=1))
        w1 = const.tile([P, 2, 768], BF16, name="w1")
        nc.sync.dma_start(out=w1[:], in_=w1o.rearrange("(j p) i m -> p j (i m)", p=P))
        load_x(0, 1)
        w2 = const.tile([P, 640], BF16, name="w2")
        nc.sync.dma_start(out=w2[:], in_=w2e.rearrange("p i m -> p (i m)"))
        load_x(0, 2)
        load_x(1, 1)
        load_x(1, 2)
        for c in range(2, len(CHUNKS)):
            load_x(c - 1, 0)
            load_x(c, 1)
            load_x(c, 2)

        bias32 = const.tile([P, 512], F32, name="bias32")

        def bias_stage():
            pb = psum.tile([P, 512], F32, name="pb", tag="b0")
            nc.tensor.matmul(pb[:], lhsT=ones[:], rhs=brow[:], start=True, stop=True)
            nc.scalar.copy(out=bias32[:], in_=pb[:])

        wg = const.tile([P, 512, 4], BF16, name="wg", align_bytes=64)
        wcodes = const.tile([P, 512], U32, name="wcodes", align_bytes=64)
        wscales = const.tile([P, 512], U8, name="wscales", align_bytes=64)

        def w0_stage(b, w0h, eng, bank):
            pw = psum.tile([P, 2, 2, P], F32, name="pw%d" % b, tag=bank)
            for j in range(2):
                wd = w0h[:, j, :].bitcast(F32)
                for u in range(2):
                    nc.tensor.transpose(pw[:, j, u, :], wd[:, u:256:2], identf[:])
            dst = wg[:, 256 * b : 256 * (b + 1), :].bitcast(F32).rearrange("p (j o) u -> p j o u", j=2)
            copy(eng, dst, pw[:].rearrange("p j u o -> p j o u"))
            nc.vector.quantize_mx(
                out=wcodes[:, 256 * b : 256 * (b + 1)].bitcast(FP8X4),
                scales=wscales[:, 256 * b : 256 * (b + 1)],
                in_=wg[:, 256 * b : 256 * (b + 1), :].rearrange("p n j -> p (n j)"),
            )

        wT1 = const.tile([P, 6, 256], BF16, name="wT1")

        def w1_stage(j, eng, bank):
            pw1 = psum.tile([P, 6, P], BF16, name="pw1_%d" % j, tag=bank)
            for m in range(3):
                for kk in range(2):
                    nc.tensor.transpose(pw1[:, 2 * m + kk, :], w1[:, j, 384 * kk + m : 384 * (kk + 1) : 3], identb[:])
            copy(eng, wT1[:, :, 128 * j : 128 * (j + 1)].bitcast(F32), pw1[:].bitcast(F32))

        wT2 = const.tile([P, 5, P], BF16, name="wT2")

        def w2_stage(eng, bank):
            pw2 = psum.tile([P, 5, P], BF16, name="pw2", tag=bank)
            for m in range(5):
                nc.tensor.transpose(pw2[:, m, :], w2[:, m:640:5], identb[:])
            copy(eng, words(wT2[:]), words(pw2[:]))

        p0s, p1s, p2s, g0s, xcs, xss, xT1s, xT2s = {}, {}, {}, {}, {}, {}, {}, {}
        ps0s, ps1s, ps2s, o32s, ams, rs, o8s = {}, {}, {}, {}, {}, {}, {}

        def x0_pe(t):
            if t % 2:
                return
            p0 = psum.tile([P, 2, 2, P], F32, name="p0", tag="b5")
            for j in range(2):
                wd = x0s[t + j].bitcast(F32)
                for u in range(2):
                    nc.tensor.transpose(p0[:, j, u, :], wd[:, u:256:2], identf[:])
            p0s[t] = p0

        def x0_cp(t, eng):
            if t % 2:
                return
            g0 = xt.tile([P, 2 * P, 4], BF16, name="g0", align_bytes=64)
            copy(
                eng,
                g0[:].bitcast(F32).rearrange("p (j n) u -> p j n u", j=2),
                p0s.pop(t)[:].rearrange("p j u n -> p j n u"),
            )
            g0s[t] = g0

        def quant(t):
            xc = xt.tile([P, P], U32, name="xc", align_bytes=64)
            xs = xt.tile([P, P], U8, name="xs", align_bytes=64)
            g0 = g0s[t - t % 2]
            nc.vector.quantize_mx(
                out=xc[:].bitcast(FP8X4),
                scales=xs[:],
                in_=g0[:, P * (t % 2) : P * (t % 2 + 1), :].rearrange("p n j -> p (n j)"),
            )
            xcs[t] = xc[:]
            xss[t] = xs[:]

        def x1_pe(t):
            p1 = psum.tile([P, 6, P], BF16, name="p1", tag="b6")
            for m in range(3):
                for kk in range(2):
                    nc.tensor.transpose(p1[:, 2 * m + kk, :], x1s[t][:, 384 * kk + m : 384 * (kk + 1) : 3], identb[:])
            p1s[t] = p1

        def x1_cp(t, eng):
            xT1 = xt.tile([P, 6, P], BF16, name="xT1")
            copy(eng, words(xT1[:]), words(p1s.pop(t)[:]))
            xT1s[t] = xT1

        def x2_pe(t):
            p2 = psum.tile([P, 5, P], BF16, name="p2", tag="b7")
            for m in range(5):
                nc.tensor.transpose(p2[:, m, :], x2s[t][:, m:640:5], identb[:])
            p2s[t] = p2

        def x2_cp(t, eng):
            xT2 = xt.tile([P, 5, P], BF16, name="xT2")
            copy(eng, words(xT2[:]), words(p2s.pop(t)[:]))
            xT2s[t] = xT2

        def m0(t):
            ps0 = psum.tile([P, 512], F32, name="ps0", tag="b0")
            nc.tensor.matmul_mx(
                out=ps0[:],
                lhsT=xcs.pop(t).bitcast(FP8X4),
                lhsT_scale=xss.pop(t),
                rhs=wcodes[:].bitcast(FP8X4),
                rhs_scale=wscales[:],
                start=True,
                stop=True,
            )
            ps0s[t] = ps0

        def m1(t):
            xT1 = xT1s.pop(t)
            pa = psum.tile([P, 3, P], F32, name="ps1a", tag="b1")
            pbk = psum.tile([P, 3, P], F32, name="ps1b", tag="b2")
            ps1 = (pa, pbk)
            for m in range(3):
                for kk in range(2):
                    for h in range(2):
                        nc.tensor.matmul(
                            ps1[h][:, m, :],
                            lhsT=xT1[:, 2 * m + kk, :],
                            rhs=wT1[:, 2 * m + kk, 128 * h : 128 * (h + 1)],
                            start=(kk == 0),
                            stop=(kk == 1),
                        )
            ps1s[t] = ps1

        def m2(t):
            xT2 = xT2s.pop(t)
            pa = psum.tile([P, 5, 64], F32, name="ps2a", tag="b3")
            pbk = psum.tile([P, 5, 64], F32, name="ps2b", tag="b4")
            ps2 = (pa, pbk)
            for m in range(5):
                for h in range(2):
                    nc.tensor.matmul(
                        ps2[h][:, m, :],
                        lhsT=xT2[:, m, :],
                        rhs=wT2[:, m, 64 * h : 64 * (h + 1)],
                        start=True,
                        stop=True,
                    )
            ps2s[t] = ps2

        def new_out(t):
            o32 = res.tile([P, 1920], F32, name="o32")
            o32s[t] = o32
            am = res.tile([P, 2], F32, name="am")
            ams[t] = am

        def a0(t):
            nc.vector.tensor_tensor(out=o32s[t][:, 0:512], in0=ps0s.pop(t)[:], in1=bias32[:], op=ALU.add)

        def a1(t, h, eng):
            copy(
                eng,
                o32s[t][:, 512 + 384 * h : 512 + 384 * (h + 1)].rearrange("p (o m) -> p o m", m=3),
                ps1s[t][h][:].rearrange("p m o -> p o m"),
            )

        def a2(t, h, eng):
            copy(
                eng,
                o32s[t][:, 1280 + 320 * h : 1280 + 320 * (h + 1)].rearrange("p (o m) -> p o m", m=5),
                ps2s[t][h][:].rearrange("p m o -> p o m"),
            )

        def st0(t):
            nc.sync.dma_start(out=o0v[:, t, :], in_=o32s[t][:])

        def red(t, piece):
            lo, hi = (((0, 1280), (1280, 1920)) if t == 0 else ((512, 1920), (0, 512)))[piece] if PIECES[t] == 2 else (0, 1920)
            nc.vector.tensor_reduce(
                out=ams[t][:, piece : piece + 1],
                in_=o32s[t][:, lo:hi],
                axis=AX.X,
                op=ALU.max,
                apply_absolute_value=True,
            )

        def factor(t):
            n = PIECES[t]
            rc = res.tile([P, 2], F32, name="rc")
            nc.vector.reciprocal(out=rc[:, 0:n], in_=ams.pop(t)[:, 0:n])
            r = res.tile([P, 1], F32, name="r")
            if t == NT - 1:
                nc.vector.tensor_scalar(
                    out=r[:], in0=rc[:, 0:1], scalar1=rc[:, 1:2], scalar2=448.0, op0=ALU.min, op1=ALU.mult
                )
            elif n == 2:
                nc.gpsimd.tensor_scalar(
                    out=r[:], in0=rc[:, 0:1], scalar1=rc[:, 1:2], scalar2=448.0, op0=ALU.min, op1=ALU.mult
                )
            else:
                nc.gpsimd.tensor_scalar(
                    out=r[:], in0=rc[:, 0:1], scalar1=448.0, scalar2=0.0, op0=ALU.mult, op1=ALU.add
                )
            rs[t] = r
            o8 = res.tile([P, 1920], FP8, name="o8")
            o8s[t] = o8

        def cast_v(t):
            cv = CVS[t]
            if cv == 0:
                return
            nc.vector.tensor_scalar(
                out=o8s[t][:, 0:cv],
                in0=o32s[t][:, 0:cv],
                scalar1=rs[t][:, 0:1],
                scalar2=None,
                op0=ALU.mult,
                saturate=False,
            )

        def cast_s(t):
            cv = CVS[t]
            nc.scalar.activation(
                out=o8s[t][:, cv:1920],
                in_=o32s[t][:, cv:1920],
                func=ACT.Identity,
                bias=zero[:, 0:1],
                scale=rs[t][:, 0:1],
                saturate=False,
            )

        def st1(t):
            nc.sync.dma_start(out=o1v[:, t, :], in_=o8s.pop(t)[:].bitcast(U8))

        w0_stage(0, w0a, "V", "b1")
        w0_stage(1, w0b, "S", "b2")
        x0_pe(0)
        x0_cp(0, "S")
        quant(0)
        bias_stage()
        w1_stage(0, "V", "b3")
        w1_stage(1, "S", "b4")
        x1_pe(0)
        x1_cp(0, "S")
        w2_stage("S", "b5")
        x2_pe(0)
        x2_cp(0, "V")
        new_out(0)
        m0(0)
        a0(0)
        m1(0)
        a1(0, 0, "S")
        a1(0, 1, "V")
        x0_pe(1)
        x0_cp(1, "S")
        quant(1)
        m2(0)
        a2(0, 0, "S")
        a2(0, 1, "V")
        st0(0)
        x1_pe(1)
        x1_cp(1, "S")
        x2_pe(1)
        x2_cp(1, "S")
        red(0, 0)
        for t in range(1, NT):
            if t + 1 < NT:
                x0_pe(t + 1)
                x1_pe(t + 1)
                x2_pe(t + 1)
            new_out(t)
            m1(t)
            m0(t)
            m2(t)
            if t + 1 < NT:
                x0_cp(t + 1, "S")
                x1_cp(t + 1, "S")
                x2_cp(t + 1, "S")
            if t >= 2:
                cast_s(t - 2)
                st1(t - 2)
            if t >= 2:
                red(t - 1, 0)
            if PIECES[t - 1] == 2:
                red(t - 1, 1)
            if t + 1 < NT:
                quant(t + 1)
            else:
                a0(t)
            factor(t - 1)
            helper = "S"
            a1(t, 0, "S")
            a1(t, 1, "S")
            if t + 1 < NT:
                a0(t)
            a2(t, 0, "S")
            a2(t, 1, helper)
            st0(t)
            cast_v(t - 1)
        cast_s(NT - 2)
        st1(NT - 2)
        red(NT - 1, 0)
        red(NT - 1, 1)
        factor(NT - 1)
        cast_v(NT - 1)
        cast_s(NT - 1)
        st1(NT - 1)
